import numpy as np
import ml_dtypes


def mxq(x, axis, fmt="e4m3"):
    dtype, down = {"e4m3": (ml_dtypes.float8_e4m3fn, 7), "e5m2": (ml_dtypes.float8_e5m2, 14)}[fmt]
    v = np.moveaxis(np.asarray(x, np.float32).astype(ml_dtypes.bfloat16).astype(np.float64), axis, -1)
    blocks = v.reshape(v.shape[:-1] + (-1, 32))
    amax = np.abs(blocks).max(-1, keepdims=True)
    byte = np.maximum(np.where(amax > 0, np.frexp(amax)[1] - 1 + 127, 0) - down, 1)
    scale = np.exp2(byte - 127.0)
    codes = (blocks / scale).astype(np.float32).astype(dtype).astype(np.float64)
    return np.moveaxis((codes * scale).reshape(v.shape), -1, axis)


WIDE = False


def mx_kscale(k):
    if not WIDE:
        return np.ones(k)
    levels = np.array([10, -10, 5, -5, 0])
    if k % 512:
        return np.exp2(np.random.permutation(np.resize(levels, k // 32))).repeat(32)
    a = np.empty((k // 512, 16))
    for p in range(k // 512):
        a[p, :8] = np.random.permutation(np.resize(levels, 8))
        for g in range(8):
            far = levels[np.abs(levels - a[p, g]) >= 10]
            a[p, g + 8] = far[np.random.randint(len(far))]
    return np.exp2(a.ravel()).repeat(32)


BF16 = ml_dtypes.bfloat16


def bf(x):
    return np.asarray(x, np.float32).astype(BF16)


def f64(x):
    return np.asarray(x).astype(np.float64)


NQ, NK, QS, KS, F, DEG = 1024, 1024, 512, 512, 512, 32
EPS = 1e-5
SLOPE = 0.01


def leaky(v):
    return np.where(v >= 0, v, SLOPE * v)


def setup_inputs():
    s, t = mx_kscale(QS), mx_kscale(F)
    return {"x": bf(np.random.standard_normal((NQ, QS)) * s),
            "w1": bf(np.random.standard_normal((QS, F)) / np.sqrt(QS) / s[:, None] * t),
            "b1": bf(np.random.standard_normal(F) * 0.5 * t),
            "w2": bf(np.random.standard_normal((F, F)) / np.sqrt(F) / t[:, None]),
            "b2": bf(np.random.standard_normal(F) * 0.5),
            "gamma": bf(1.0 + 0.1 * np.random.standard_normal(F)),
            "beta": bf(0.1 * np.random.standard_normal(F))}


def reference(x, w1, b1, w2, b2, gamma, beta):
    h = leaky((mxq(f64(x), 1, "e4m3") @ mxq(f64(w1), 0, "e4m3")) + f64(b1))
    h = leaky((mxq(h, 1, "e4m3") @ mxq(f64(w2), 0, "e4m3")) + f64(b2))
    mean = h.mean(axis=0)
    var = h.var(axis=0)
    return f64(gamma) * (h - mean) / np.sqrt(var + EPS) + f64(beta)

@@ -1,0 +1,506 @@
+from contextlib import ExitStack
+
+import concourse.mybir as mybir
+from concourse.masks import make_identity
+
+F32 = mybir.dt.float32
+BF16 = mybir.dt.bfloat16
+U32 = mybir.dt.uint32
+U8 = mybir.dt.uint8
+FP8X4 = mybir.dt.float8_e4m3fn_x4
+ALU = mybir.AluOpType
+ACT = mybir.ActivationFunctionType
+
+P = 128
+ROWS = 1024
+WIDTH = 512
+PACK = 4
+STRIPES = ROWS // P
+PIECE = 256
+HALF = 512
+HALVES = ROWS // HALF
+W1_PART = 256
+RUN = 4
+BN_STATS_SIZE = 6
+BANKS = 8
+EPS = 1e-5
+SLOPE = 0.01
+
+FLOPS = 2 * 2 * ROWS * WIDTH * WIDTH
+
+
+def tile_attention_prop_pa_kernel(tc, x, w1, b1, w2, b2, gamma, beta, out):
+    nc = tc.nc
+    with ExitStack() as ctx:
+        sbuf = ctx.enter_context(tc.tile_pool(name="sbuf", bufs=1))
+        psum = ctx.enter_context(tc.psum_pool(name="psum", bufs=1))
+        ctx.enter_context(tc.manual_schedule())
+
+        banks_taken = [0]
+
+        def next_bank(shape, name):
+            tag = "bank%d" % (banks_taken[0] % BANKS)
+            banks_taken[0] = banks_taken[0] + 1
+            return psum.tile(shape, F32, tag=tag, name=name)
+
+        b1_col = sbuf.tile([P, PACK], BF16, name="b1_col")
+        rest_rows = sbuf.tile([P, P], BF16, name="rest_rows")
+        nc.vector.memset(rest_rows[:], 0.0)
+        one = sbuf.tile([P, 1], F32, name="one")
+        nc.vector.memset(one[:], 1.0)
+        nc.scalar.dma_start(out=b1_col[:], in_=b1.rearrange("(p t) -> p t", t=PACK))
+        table_warmer = sbuf.tile([P, 1], F32, name="table_warmer")
+        nc.scalar.activation(out=table_warmer[:], in_=one[:], func=ACT.Abs_reciprocal_sqrt)
+        identity = sbuf.tile([P, P], F32, name="identity")
+        make_identity(nc, identity[:])
+        for r, values in enumerate((b2, gamma, beta)):
+            nc.gpsimd.dma_start(
+                out=rest_rows[PACK * r : PACK * (r + 1), :], in_=values.rearrange("(t p) -> t p", p=P)
+            )
+
+        x_view = x.rearrange("(i c) k -> i (c k)", c=STRIPES)
+        stripes_in_piece = PIECE // P
+        x_share = stripes_in_piece * WIDTH
+        w_view = {
+            "w1": w1.rearrange("(p t) f -> p t f", t=PACK),
+            "w2": w2.rearrange("(p t) f -> p t f", t=PACK),
+        }
+        x_raw = {}
+        w_raw = {}
+
+        def load_x(piece):
+            x_raw[piece] = sbuf.tile([P, x_share], BF16, name="x_raw%d" % piece)
+            nc.sync.dma_start(out=x_raw[piece][:], in_=x_view[:, x_share * piece : x_share * (piece + 1)])
+
+        def load_w(part):
+            w_raw[part] = sbuf.tile([P, PACK, WIDTH], BF16, name="raw_" + part)
+            nc.sync.dma_start(out=w_raw[part][:], in_=w_view[part])
+
+        load_x(0)
+        load_w("w1")
+        load_x(1)
+        load_x(2)
+        load_w("w2")
+        load_x(3)
+
+        w1_words = sbuf.tile([P, WIDTH], U32, align_bytes=64, name="w1_words")
+        w1_plane = sbuf.tile([P, WIDTH], U8, align_bytes=64, name="w1_plane")
+        w2_words = sbuf.tile([P, WIDTH], U32, align_bytes=64, name="w2_words")
+        w2_plane = sbuf.tile([P, WIDTH], U8, align_bytes=64, name="w2_plane")
+        x_words = sbuf.tile([P, ROWS], U32, align_bytes=64, name="x_words")
+        x_plane = sbuf.tile([P, ROWS], U8, align_bytes=64, name="x_plane")
+        h1_words = sbuf.tile([P, ROWS], U32, align_bytes=64, name="h1_words")
+        h1_plane = sbuf.tile([P, ROWS], U8, align_bytes=64, name="h1_plane")
+        w_packed = {
+            "w1a": (w1_words[:, 0:W1_PART], w1_plane[:, 0:W1_PART]),
+            "w1b": (w1_words[:, W1_PART:WIDTH], w1_plane[:, W1_PART:WIDTH]),
+            "w2": (w2_words[:], w2_plane[:]),
+        }
+
+        w_grouped = {}
+
+        def regroup_w1(part):
+            first = {"w1a": 0, "w1b": W1_PART // P}[part]
+            groups = W1_PART // P
+            w_grouped[part] = sbuf.tile([P, W1_PART, PACK], BF16, align_bytes=64, name="grouped_" + part)
+            nc.vector.tensor_copy(
+                out=w_grouped[part][:].rearrange("p (t m) k -> p t m k", t=groups),
+                in_=w_raw["w1"][:].rearrange("p k (m t) -> p t m k", t=PACK)[:, first : first + groups],
+            )
+
+        def regroup_w2():
+            w_grouped["w2"] = sbuf.tile([P, WIDTH, PACK], BF16, align_bytes=64, name="grouped_w2")
+            nc.vector.tensor_copy(
+                out=w_grouped["w2"][:].rearrange("p (b r) t -> p b t r", r=RUN),
+                in_=w_raw["w2"][:].rearrange("p t (b r) -> p b t r", r=RUN),
+            )
+
+        def quantise_w(part):
+            words, plane = w_packed[part]
+            nc.vector.quantize_mx(
+                out=words.bitcast(FP8X4), scales=plane, in_=w_grouped[part][:].rearrange("p f t -> p (f t)")
+            )
+
+        x_bank = {}
+        x_grouped = {}
+
+        def transpose_x(piece):
+            x_bank[piece] = next_bank([P, stripes_in_piece, 2, P], "x_bank%d" % piece)
+            x_as_f32 = x_raw[piece][:].bitcast(F32).rearrange("i (c p u) -> i c u p", c=stripes_in_piece, u=2)
+            for c in range(stripes_in_piece):
+                for u in range(2):
+                    nc.tensor.transpose(x_bank[piece][:, c, u, :], x_as_f32[:, c, u, :], identity[:])
+
+        def copy_x(piece):
+            x_grouped[piece] = sbuf.tile([P, PACK * PIECE], BF16, align_bytes=64, name="x_grouped%d" % piece)
+            nc.scalar.copy(
+                out=x_grouped[piece][:].bitcast(F32).rearrange("p (c i u) -> p c i u", c=stripes_in_piece, u=2),
+                in_=x_bank[piece][:].rearrange("p c u i -> p c i u"),
+            )
+
+        def piece_columns(piece):
+            return slice(PIECE * piece, PIECE * (piece + 1))
+
+        def quantise_x(piece):
+            cols = piece_columns(piece)
+            nc.vector.quantize_mx(
+                out=x_words[:, cols].bitcast(FP8X4), scales=x_plane[:, cols], in_=x_grouped[piece][:]
+            )
+
+        small_bank = {}
+
+        rest_f32 = sbuf.tile([P, P], F32, name="rest_f32")
+        rest_col = sbuf.tile([P, 3 * PACK], F32, name="rest_col")
+        b2_most = sbuf.tile([P, PACK], F32, name="b2_most")
+        centre = sbuf.tile([P, PACK], F32, name="centre")
+        minus_centre = sbuf.tile([P, PACK], F32, name="minus_centre")
+        gamma_signed = sbuf.tile([P, PACK, 2], F32, name="gamma_signed")
+
+        def beta_col(chunk):
+            return rest_col[:, 2 * PACK + chunk : 2 * PACK + chunk + 1]
+
+        def cast_rest():
+            nc.scalar.copy(out=rest_f32[:], in_=rest_rows[:])
+
+        def transpose_rest():
+            small_bank["rest"] = next_bank([P, P], "rest_bank")
+            nc.tensor.transpose(small_bank["rest"][:], rest_f32[:], identity[:])
+
+        def derive_rest():
+            nc.scalar.copy(out=rest_col[:], in_=small_bank["rest"][:, 0 : 3 * PACK])
+            nc.scalar.mul(out=b2_most[:], in_=rest_col[:, 0:PACK], mul=1.0 - SLOPE)
+            nc.scalar.copy(out=gamma_signed[:, :, 0], in_=rest_col[:, PACK : 2 * PACK])
+            nc.scalar.mul(out=gamma_signed[:, :, 1], in_=rest_col[:, PACK : 2 * PACK], mul=-1.0)
+            nc.scalar.activation(out=centre[:], in_=b2_most[:], func=ACT.Relu)
+            nc.scalar.mul(out=minus_centre[:], in_=centre[:], mul=-1.0)
+
+        l1_bank = {}
+        v = {}
+        h1_grouped = {}
+
+        def layer1(piece, pair):
+            cols = piece_columns(piece)
+            l1_bank[piece, pair] = next_bank([P, 2, PIECE], "l1_bank%d_%d" % (piece, pair))
+            for e in range(2):
+                features = slice(P * (2 * pair + e), P * (2 * pair + e + 1))
+                nc.tensor.matmul_mx(
+                    out=l1_bank[piece, pair][:, e, :],
+                    lhsT=w1_words[:, features].bitcast(FP8X4),
+                    lhsT_scale=w1_plane[:, features],
+                    rhs=x_words[:, cols].bitcast(FP8X4),
+                    rhs_scale=x_plane[:, cols],
+                    start=True,
+                    stop=True,
+                )
+
+        def add_b1(piece):
+            v[piece] = sbuf.tile([P, PACK, PIECE], F32, name="v%d" % piece)
+            for t in range(PACK):
+                nc.scalar.activation(
+                    out=v[piece][:, t, :],
+                    in_=l1_bank[piece, t // 2][:, t % 2, :],
+                    func=ACT.Identity,
+                    bias=b1_col[:, t : t + 1],
+                    scale=1.0,
+                )
+
+        def leaky1(piece):
+            h1_grouped[piece] = sbuf.tile([P, PIECE, PACK], BF16, align_bytes=64, name="h1_grouped%d" % piece)
+            by_row = v[piece][:].rearrange("p t n -> p n t")
+            nc.vector.scalar_tensor_tensor(
+                out=h1_grouped[piece][:], in0=by_row, scalar=SLOPE, in1=by_row, op0=ALU.mult, op1=ALU.max
+            )
+
+        def quantise_h1(piece):
+            cols = piece_columns(piece)
+            nc.vector.quantize_mx(
+                out=h1_words[:, cols].bitcast(FP8X4),
+                scales=h1_plane[:, cols],
+                in_=h1_grouped[piece][:].rearrange("p n t -> p (n t)"),
+            )
+
+        def half_columns(half):
+            return slice(HALF * half, HALF * (half + 1))
+
+        l2_bank = {}
+        sloped = {}
+        q = {}
+
+        def layer2(chunk, half):
+            features = slice(P * chunk, P * (chunk + 1))
+            cols = half_columns(half)
+            l2_bank[chunk, half] = next_bank([P, HALF], "l2_bank%d_%d" % (chunk, half))
+            nc.tensor.matmul_mx(
+                out=l2_bank[chunk, half][:],
+                lhsT=w2_words[:, features].bitcast(FP8X4),
+                lhsT_scale=w2_plane[:, features],
+                rhs=h1_words[:, cols].bitcast(FP8X4),
+                rhs_scale=h1_plane[:, cols],
+                start=True,
+                stop=True,
+            )
+
+        def slope2(chunk, half):
+            sloped[chunk, half] = sbuf.tile([P, HALF], F32, name="sloped%d_%d" % (chunk, half))
+            nc.scalar.mul(out=sloped[chunk, half][:], in_=l2_bank[chunk, half][:], mul=SLOPE)
+
+        def leaky2(chunk, half, row_sum=None):
+            if chunk not in q:
+                q[chunk] = sbuf.tile([P, ROWS], F32, name="q%d" % chunk)
+            nc.vector.scalar_tensor_tensor(
+                out=q[chunk][:, half_columns(half)],
+                in0=l2_bank[chunk, half][:],
+                scalar=b2_most[:, chunk : chunk + 1],
+                in1=sloped[chunk, half][:],
+                op0=ALU.add,
+                op1=ALU.max,
+                accum_out=row_sum,
+            )
+
+        half_stats = {}
+        moments = {}
+
+        def stats_on_vector(chunk, half):
+            if chunk not in half_stats:
+                half_stats[chunk] = sbuf.tile([P, HALVES, BN_STATS_SIZE], F32, name="half_stats%d" % chunk)
+            nc.vector.bn_stats(out=half_stats[chunk][:, half, :], in_=q[chunk][:, half_columns(half)])
+
+        def moments_on_vector(chunk):
+            moments[chunk] = sbuf.tile([P, 2], F32, name="moments%d" % chunk)
+            nc.vector.bn_aggr(out=moments[chunk][:], in_=half_stats[chunk][:].rearrange("p h s -> p (h s)"))
+
+        sums = sbuf.tile([P, HALVES], F32, name="sums")
+        squares = sbuf.tile([P, HALVES], F32, name="squares")
+
+        def squares_on_scalar(chunk, half):
+            unused = sbuf.tile([P, HALF], BF16, name="unused%d" % half)
+            nc.scalar.activation(
+                out=unused[:],
+                in_=q[chunk][:, half_columns(half)],
+                func=ACT.Square,
+                bias=minus_centre[:, chunk : chunk + 1],
+                scale=1.0,
+                accum_out=squares[:, half : half + 1],
+            )
+
+        def moments_on_gpsimd(chunk):
+            moments[chunk] = sbuf.tile([P, 2], F32, name="moments%d" % chunk)
+            work = sbuf.tile([P, 2], F32, name="moments_work")
+            nc.gpsimd.tensor_scalar(
+                out=moments[chunk][:, 0:1],
+                in0=sums[:, 0:1],
+                scalar1=sums[:, 1:2],
+                scalar2=1.0 / ROWS,
+                op0=ALU.add,
+                op1=ALU.mult,
+            )
+            nc.gpsimd.tensor_scalar(
+                out=work[:, 0:1],
+                in0=squares[:, 0:1],
+                scalar1=squares[:, 1:2],
+                scalar2=1.0 / ROWS,
+                op0=ALU.add,
+                op1=ALU.mult,
+            )
+            nc.gpsimd.tensor_scalar(
+                out=work[:, 1:2],
+                in0=moments[chunk][:, 0:1],
+                scalar1=minus_centre[:, chunk : chunk + 1],
+                scalar2=0.0,
+                op0=ALU.add,
+                op1=ALU.add,
+            )
+            nc.gpsimd.tensor_scalar(
+                out=moments[chunk][:, 1:2],
+                in0=work[:, 1:2],
+                scalar1=work[:, 1:2],
+                scalar2=work[:, 0:1],
+                op0=ALU.mult,
+                op1=ALU.subtract,
+            )
+
+        inverse_deviation = {}
+        gain = {}
+        shift = {}
+
+        def invert_deviation(chunk, variance_sign):
+            inverse_deviation[chunk] = sbuf.tile([P, 1], F32, name="inverse_deviation%d" % chunk)
+            nc.scalar.activation(
+                out=inverse_deviation[chunk][:],
+                in_=moments[chunk][:, 1:2],
+                func=ACT.Abs_reciprocal_sqrt,
+                bias=EPS,
+                scale=variance_sign,
+            )
+
+        def gain_and_shift(chunk, engine):
+            gain[chunk] = sbuf.tile([P, 2], F32, name="gain%d" % chunk)
+            shift[chunk] = sbuf.tile([P, 1], F32, name="shift%d" % chunk)
+            engine.tensor_scalar(
+                out=gain[chunk][:],
+                in0=gamma_signed[:, chunk, :],
+                scalar1=inverse_deviation[chunk][:, 0:1],
+                scalar2=0.0,
+                op0=ALU.mult,
+                op1=ALU.add,
+            )
+            engine.tensor_scalar(
+                out=shift[chunk][:],
+                in0=moments[chunk][:, 0:1],
+                scalar1=gain[chunk][:, 1:2],
+                scalar2=beta_col(chunk),
+                op0=ALU.mult,
+                op1=ALU.add,
+            )
+
+        y = {}
+
+        def normalise(chunk, half, engine):
+            if chunk not in y:
+                y[chunk] = sbuf.tile([P, ROWS], F32, name="y%d" % chunk)
+            cols = half_columns(half)
+            if engine is nc.scalar:
+                engine.activation(
+                    out=y[chunk][:, cols],
+                    in_=q[chunk][:, cols],
+                    func=ACT.Identity,
+                    bias=shift[chunk][:, 0:1],
+                    scale=gain[chunk][:, 0:1],
+                )
+            else:
+                engine.tensor_scalar(
+                    out=y[chunk][:, cols],
+                    in0=q[chunk][:, cols],
+                    scalar1=gain[chunk][:, 0:1],
+                    scalar2=shift[chunk][:, 0:1],
+                    op0=ALU.mult,
+                    op1=ALU.add,
+                )
+
+        out_bank = {}
+        out_view = out.rearrange("(i c) f -> i c f", c=STRIPES)
+        stripes_in_half = HALF // P
+
+        def transpose_out(chunk, half):
+            out_bank[chunk, half] = next_bank([P, stripes_in_half, P], "out_bank%d_%d" % (chunk, half))
+            for c in range(stripes_in_half):
+                first = HALF * half + P * c
+                nc.tensor.transpose(out_bank[chunk, half][:, c, :], y[chunk][:, first : first + P], identity[:])
+
+        def copy_and_store(chunk, half, engine):
+            rows = sbuf.tile([P, stripes_in_half, P], F32, name="rows%d_%d" % (chunk, half))
+            if engine is nc.scalar:
+                engine.copy(out=rows[:], in_=out_bank[chunk, half][:])
+            else:
+                engine.tensor_copy(out=rows[:], in_=out_bank[chunk, half][:])
+            stripes = slice(stripes_in_half * half, stripes_in_half * (half + 1))
+            nc.sync.dma_start(out=out_view[:, stripes, P * chunk : P * (chunk + 1)], in_=rows[:])
+
+        scalar, vector, gpsimd = nc.scalar, nc.vector, nc.gpsimd
+
+        transpose_x(0)
+        copy_x(0)
+        regroup_w1("w1a")
+        quantise_x(0)
+        quantise_w("w1a")
+        transpose_x(1)
+        copy_x(1)
+        regroup_w1("w1b")
+        quantise_x(1)
+        quantise_w("w1b")
+        transpose_x(2)
+        copy_x(2)
+        regroup_w2()
+        quantise_x(2)
+        quantise_w("w2")
+
+        layer1(0, 0)
+        layer1(0, 1)
+        add_b1(0)
+        transpose_x(3)
+        copy_x(3)
+        leaky1(0)
+        quantise_x(3)
+        quantise_h1(0)
+        for piece in (1, 2, 3):
+            layer1(piece, 0)
+            layer1(piece, 1)
+            add_b1(piece)
+        leaky1(1)
+        quantise_h1(1)
+        leaky1(2)
+        leaky1(3)
+        quantise_h1(2)
+        quantise_h1(3)
+
+        cast_rest()
+        layer2(0, 0)
+        layer2(1, 0)
+        transpose_rest()
+        slope2(0, 0)
+        derive_rest()
+        slope2(1, 0)
+        layer2(2, 0)
+        slope2(2, 0)
+        leaky2(0, 0)
+        leaky2(1, 0, row_sum=sums[:, 0:1])
+        stats_on_vector(0, 0)
+        layer2(0, 1)
+        layer2(1, 1)
+        slope2(0, 1)
+        slope2(1, 1)
+        leaky2(0, 1)
+        leaky2(1, 1, row_sum=sums[:, 1:2])
+        stats_on_vector(0, 1)
+        squares_on_scalar(1, 0)
+        layer2(2, 1)
+        slope2(2, 1)
+        squares_on_scalar(1, 1)
+        leaky2(2, 0)
+        moments_on_vector(0)
+        leaky2(2, 1)
+        moments_on_gpsimd(1)
+        invert_deviation(0, 1.0)
+        gain_and_shift(0, vector)
+        stats_on_vector(2, 0)
+        stats_on_vector(2, 1)
+        layer2(3, 0)
+        slope2(3, 0)
+        normalise(0, 0, scalar)
+        normalise(0, 1, gpsimd)
+        invert_deviation(1, -1.0)
+        gain_and_shift(1, vector)
+        layer2(3, 1)
+        slope2(3, 1)
+        normalise(1, 0, scalar)
+        normalise(1, 1, gpsimd)
+        moments_on_vector(2)
+        leaky2(3, 0)
+        leaky2(3, 1)
+        invert_deviation(2, 1.0)
+        gain_and_shift(2, gpsimd)
+        stats_on_vector(3, 0)
+        stats_on_vector(3, 1)
+
+        for chunk in (0, 1):
+            for half in (0, 1):
+                transpose_out(chunk, half)
+        copy_and_store(0, 0, scalar)
+        copy_and_store(0, 1, scalar)
+        copy_and_store(1, 0, scalar)
+        normalise(2, 0, gpsimd)
+        normalise(2, 1, vector)
+        moments_on_vector(3)
+        copy_and_store(1, 1, vector)
+        invert_deviation(3, 1.0)
+        gain_and_shift(3, vector)
+        transpose_out(2, 0)
+        transpose_out(2, 1)
+        copy_and_store(2, 0, scalar)
+        copy_and_store(2, 1, scalar)
+        normalise(3, 0, vector)
+        normalise(3, 1, vector)
+        transpose_out(3, 0)
+        transpose_out(3, 1)
+        copy_and_store(3, 0, vector)
+        copy_and_store(3, 1, scalar)

@@ -19,6 +19,8 @@ STRIPES = ROWS // P
 PIECE = 256
 HALF = 512
 HALVES = ROWS // HALF
+QUARTER = 256
+W1_COLS = 256
 W1_PART = 256
 RUN = 4
 BN_STATS_SIZE = 6
@@ -62,9 +64,11 @@ def tile_attention_prop_pa_kernel(tc, x, w1, b1, w2, b2, gamma, beta, out):
         stripes_in_piece = PIECE // P
         x_share = stripes_in_piece * WIDTH
         w_view = {
-            "w1": w1.rearrange("(p t) f -> p t f", t=PACK),
+            "w1l": w1.rearrange("(p t) f -> p t f", t=PACK)[:, :, 0:W1_COLS],
+            "w1r": w1.rearrange("(p t) f -> p t f", t=PACK)[:, :, W1_COLS:WIDTH],
             "w2": w2.rearrange("(p t) f -> p t f", t=PACK),
         }
+        w_width = {"w1l": W1_COLS, "w1r": WIDTH - W1_COLS, "w2": WIDTH}
         x_raw = {}
         w_raw = {}
 
@@ -73,14 +77,15 @@ def tile_attention_prop_pa_kernel(tc, x, w1, b1, w2, b2, gamma, beta, out):
             nc.sync.dma_start(out=x_raw[piece][:], in_=x_view[:, x_share * piece : x_share * (piece + 1)])
 
         def load_w(part):
-            w_raw[part] = sbuf.tile([P, PACK, WIDTH], BF16, name="raw_" + part)
+            w_raw[part] = sbuf.tile([P, PACK, w_width[part]], BF16, name="raw_" + part)
             nc.sync.dma_start(out=w_raw[part][:], in_=w_view[part])
 
         load_x(0)
-        load_w("w1")
+        load_w("w1l")
+        load_w("w1r")
         load_x(1)
-        load_x(2)
         load_w("w2")
+        load_x(2)
         load_x(3)
 
         w1_words = sbuf.tile([P, WIDTH], U32, align_bytes=64, name="w1_words")
@@ -91,34 +96,31 @@ def tile_attention_prop_pa_kernel(tc, x, w1, b1, w2, b2, gamma, beta, out):
         x_plane = sbuf.tile([P, ROWS], U8, align_bytes=64, name="x_plane")
         h1_words = sbuf.tile([P, ROWS], U32, align_bytes=64, name="h1_words")
         h1_plane = sbuf.tile([P, ROWS], U8, align_bytes=64, name="h1_plane")
+        w1_grouped = sbuf.tile([P, WIDTH, PACK], BF16, align_bytes=64, name="w1_grouped")
+        w2_grouped = sbuf.tile([P, WIDTH, PACK], BF16, align_bytes=64, name="w2_grouped")
         w_packed = {
-            "w1a": (w1_words[:, 0:W1_PART], w1_plane[:, 0:W1_PART]),
-            "w1b": (w1_words[:, W1_PART:WIDTH], w1_plane[:, W1_PART:WIDTH]),
-            "w2": (w2_words[:], w2_plane[:]),
+            "w1a": (w1_words[:, 0:W1_PART], w1_plane[:, 0:W1_PART], w1_grouped[:, 0:W1_PART, :]),
+            "w1b": (w1_words[:, W1_PART:WIDTH], w1_plane[:, W1_PART:WIDTH], w1_grouped[:, W1_PART:WIDTH, :]),
+            "w2": (w2_words[:], w2_plane[:], w2_grouped[:]),
         }
 
-        w_grouped = {}
-
         def regroup_w1(part):
-            first = {"w1a": 0, "w1b": W1_PART // P}[part]
-            groups = W1_PART // P
-            w_grouped[part] = sbuf.tile([P, W1_PART, PACK], BF16, align_bytes=64, name="grouped_" + part)
+            ms = {"w1l": slice(0, P // 2), "w1r": slice(P // 2, P)}[part]
             nc.vector.tensor_copy(
-                out=w_grouped[part][:].rearrange("p (t m) k -> p t m k", t=groups),
-                in_=w_raw["w1"][:].rearrange("p k (m t) -> p t m k", t=PACK)[:, first : first + groups],
+                out=w1_grouped[:].rearrange("p (t m) k -> p t m k", t=PACK)[:, :, ms, :],
+                in_=w_raw[part][:].rearrange("p k (m t) -> p t m k", t=PACK),
             )
 
         def regroup_w2():
-            w_grouped["w2"] = sbuf.tile([P, WIDTH, PACK], BF16, align_bytes=64, name="grouped_w2")
             nc.vector.tensor_copy(
-                out=w_grouped["w2"][:].rearrange("p (b r) t -> p b t r", r=RUN),
+                out=w2_grouped[:].rearrange("p (b r) t -> p b t r", r=RUN),
                 in_=w_raw["w2"][:].rearrange("p t (b r) -> p b t r", r=RUN),
             )
 
         def quantise_w(part):
-            words, plane = w_packed[part]
+            words, plane, grouped = w_packed[part]
             nc.vector.quantize_mx(
-                out=words.bitcast(FP8X4), scales=plane, in_=w_grouped[part][:].rearrange("p f t -> p (f t)")
+                out=words.bitcast(FP8X4), scales=plane, in_=grouped.rearrange("p f t -> p (f t)")
             )
 
         x_bank = {}
@@ -153,8 +155,9 @@ def tile_attention_prop_pa_kernel(tc, x, w1, b1, w2, b2, gamma, beta, out):
         rest_col = sbuf.tile([P, 3 * PACK], F32, name="rest_col")
         b2_most = sbuf.tile([P, PACK], F32, name="b2_most")
         centre = sbuf.tile([P, PACK], F32, name="centre")
-        minus_centre = sbuf.tile([P, PACK], F32, name="minus_centre")
-        gamma_signed = sbuf.tile([P, PACK, 2], F32, name="gamma_signed")
+
+        def gamma_col(chunk):
+            return rest_col[:, PACK + chunk : PACK + chunk + 1]
 
         def beta_col(chunk):
             return rest_col[:, 2 * PACK + chunk : 2 * PACK + chunk + 1]
@@ -169,10 +172,7 @@ def tile_attention_prop_pa_kernel(tc, x, w1, b1, w2, b2, gamma, beta, out):
         def derive_rest():
             nc.scalar.copy(out=rest_col[:], in_=small_bank["rest"][:, 0 : 3 * PACK])
             nc.scalar.mul(out=b2_most[:], in_=rest_col[:, 0:PACK], mul=1.0 - SLOPE)
-            nc.scalar.copy(out=gamma_signed[:, :, 0], in_=rest_col[:, PACK : 2 * PACK])
-            nc.scalar.mul(out=gamma_signed[:, :, 1], in_=rest_col[:, PACK : 2 * PACK], mul=-1.0)
-            nc.scalar.activation(out=centre[:], in_=b2_most[:], func=ACT.Relu)
-            nc.scalar.mul(out=minus_centre[:], in_=centre[:], mul=-1.0)
+            nc.scalar.activation(out=centre[:], in_=rest_col[:, 0:PACK], func=ACT.Relu, scale=1.0 - SLOPE)
 
         l1_bank = {}
         v = {}
@@ -278,8 +278,8 @@ def tile_attention_prop_pa_kernel(tc, x, w1, b1, w2, b2, gamma, beta, out):
                 out=unused[:],
                 in_=q[chunk][:, half_columns(half)],
                 func=ACT.Square,
-                bias=minus_centre[:, chunk : chunk + 1],
-                scale=1.0,
+                bias=centre[:, chunk : chunk + 1],
+                scale=-1.0,
                 accum_out=squares[:, half : half + 1],
             )
 
@@ -305,9 +305,9 @@ def tile_attention_prop_pa_kernel(tc, x, w1, b1, w2, b2, gamma, beta, out):
             nc.gpsimd.tensor_scalar(
                 out=work[:, 1:2],
                 in0=moments[chunk][:, 0:1],
-                scalar1=minus_centre[:, chunk : chunk + 1],
+                scalar1=centre[:, chunk : chunk + 1],
                 scalar2=0.0,
-                op0=ALU.add,
+                op0=ALU.subtract,
                 op1=ALU.add,
             )
             nc.gpsimd.tensor_scalar(
@@ -320,8 +320,20 @@ def tile_attention_prop_pa_kernel(tc, x, w1, b1, w2, b2, gamma, beta, out):
             )
 
         inverse_deviation = {}
+        mean_gamma = {}
         gain = {}
         shift = {}
+
+        def weigh_mean(chunk, engine):
+            mean_gamma[chunk] = sbuf.tile([P, 1], F32, name="mean_gamma%d" % chunk)
+            engine.tensor_scalar(
+                out=mean_gamma[chunk][:],
+                in0=moments[chunk][:, 0:1],
+                scalar1=gamma_col(chunk),
+                scalar2=-1.0,
+                op0=ALU.mult,
+                op1=ALU.mult,
+            )
 
         def invert_deviation(chunk, variance_sign):
             inverse_deviation[chunk] = sbuf.tile([P, 1], F32, name="inverse_deviation%d" % chunk)
@@ -334,20 +346,20 @@ def tile_attention_prop_pa_kernel(tc, x, w1, b1, w2, b2, gamma, beta, out):
             )
 
         def gain_and_shift(chunk, engine):
-            gain[chunk] = sbuf.tile([P, 2], F32, name="gain%d" % chunk)
+            gain[chunk] = sbuf.tile([P, 1], F32, name="gain%d" % chunk)
             shift[chunk] = sbuf.tile([P, 1], F32, name="shift%d" % chunk)
             engine.tensor_scalar(
                 out=gain[chunk][:],
-                in0=gamma_signed[:, chunk, :],
-                scalar1=inverse_deviation[chunk][:, 0:1],
+                in0=gamma_col(chunk),
+                scalar1=inverse_deviation[chunk][:],
                 scalar2=0.0,
                 op0=ALU.mult,
                 op1=ALU.add,
             )
             engine.tensor_scalar(
                 out=shift[chunk][:],
-                in0=moments[chunk][:, 0:1],
-                scalar1=gain[chunk][:, 1:2],
+                in0=mean_gamma[chunk][:],
+                scalar1=inverse_deviation[chunk][:],
                 scalar2=beta_col(chunk),
                 op0=ALU.mult,
                 op1=ALU.add,
@@ -355,79 +367,83 @@ def tile_attention_prop_pa_kernel(tc, x, w1, b1, w2, b2, gamma, beta, out):
 
         y = {}
 
-        def normalise(chunk, half, engine):
+        def normalise(chunk, half, engine, quarter=None):
             if chunk not in y:
                 y[chunk] = sbuf.tile([P, ROWS], F32, name="y%d" % chunk)
-            cols = half_columns(half)
+            cols = half_columns(half) if quarter is None else slice(QUARTER * quarter, QUARTER * (quarter + 1))
             if engine is nc.scalar:
                 engine.activation(
                     out=y[chunk][:, cols],
                     in_=q[chunk][:, cols],
                     func=ACT.Identity,
-                    bias=shift[chunk][:, 0:1],
-                    scale=gain[chunk][:, 0:1],
+                    bias=shift[chunk][:],
+                    scale=gain[chunk][:],
                 )
             else:
                 engine.tensor_scalar(
                     out=y[chunk][:, cols],
                     in0=q[chunk][:, cols],
-                    scalar1=gain[chunk][:, 0:1],
-                    scalar2=shift[chunk][:, 0:1],
+                    scalar1=gain[chunk][:],
+                    scalar2=shift[chunk][:],
                     op0=ALU.mult,
                     op1=ALU.add,
                 )
 
         out_bank = {}
         out_view = out.rearrange("(i c) f -> i c f", c=STRIPES)
-        stripes_in_half = HALF // P
 
-        def transpose_out(chunk, half):
-            out_bank[chunk, half] = next_bank([P, stripes_in_half, P], "out_bank%d_%d" % (chunk, half))
-            for c in range(stripes_in_half):
-                first = HALF * half + P * c
-                nc.tensor.transpose(out_bank[chunk, half][:, c, :], y[chunk][:, first : first + P], identity[:])
+        def transpose_out(chunk, first, count):
+            out_bank[chunk, first] = next_bank([P, count, P], "out_bank%d_%d" % (chunk, first))
+            for c in range(count):
+                row = P * (first + c)
+                nc.tensor.transpose(out_bank[chunk, first][:, c, :], y[chunk][:, row : row + P], identity[:])
 
-        def copy_and_store(chunk, half, engine):
-            rows = sbuf.tile([P, stripes_in_half, P], F32, name="rows%d_%d" % (chunk, half))
+        def copy_and_store(chunk, first, count, engine):
+            rows = sbuf.tile([P, count, P], F32, name="rows%d_%d" % (chunk, first))
             if engine is nc.scalar:
-                engine.copy(out=rows[:], in_=out_bank[chunk, half][:])
+                engine.copy(out=rows[:], in_=out_bank[chunk, first][:])
             else:
-                engine.tensor_copy(out=rows[:], in_=out_bank[chunk, half][:])
-            stripes = slice(stripes_in_half * half, stripes_in_half * (half + 1))
-            nc.sync.dma_start(out=out_view[:, stripes, P * chunk : P * (chunk + 1)], in_=rows[:])
+                engine.tensor_copy(out=rows[:], in_=out_bank[chunk, first][:])
+            nc.sync.dma_start(
+                out=out_view[:, first : first + count, P * chunk : P * (chunk + 1)], in_=rows[:]
+            )
 
         scalar, vector, gpsimd = nc.scalar, nc.vector, nc.gpsimd
 
         transpose_x(0)
         copy_x(0)
-        regroup_w1("w1a")
+        regroup_w1("w1l")
+        regroup_w1("w1r")
         quantise_x(0)
         quantise_w("w1a")
+        quantise_w("w1b")
         transpose_x(1)
         copy_x(1)
-        regroup_w1("w1b")
-        quantise_x(1)
-        quantise_w("w1b")
-        transpose_x(2)
-        copy_x(2)
         regroup_w2()
-        quantise_x(2)
-        quantise_w("w2")
-
+        quantise_x(1)
         layer1(0, 0)
         layer1(0, 1)
         add_b1(0)
+        quantise_w("w2")
+        transpose_x(2)
+        copy_x(2)
+        layer1(1, 0)
+        layer1(1, 1)
+        leaky1(0)
+        add_b1(1)
+        quantise_x(2)
+        quantise_h1(0)
         transpose_x(3)
         copy_x(3)
-        leaky1(0)
-        quantise_x(3)
-        quantise_h1(0)
-        for piece in (1, 2, 3):
-            layer1(piece, 0)
-            layer1(piece, 1)
-            add_b1(piece)
+        layer1(2, 0)
+        layer1(2, 1)
+        add_b1(2)
         leaky1(1)
+        quantise_x(3)
         quantise_h1(1)
+        layer1(3, 0)
+        layer1(3, 1)
+        add_b1(3)
         leaky1(2)
         leaky1(3)
         quantise_h1(2)
@@ -459,7 +475,9 @@ def tile_attention_prop_pa_kernel(tc, x, w1, b1, w2, b2, gamma, beta, out):
         leaky2(2, 0)
         moments_on_vector(0)
         leaky2(2, 1)
+        weigh_mean(0, vector)
         moments_on_gpsimd(1)
+        weigh_mean(1, gpsimd)
         invert_deviation(0, 1.0)
         gain_and_shift(0, vector)
         stats_on_vector(2, 0)
@@ -477,6 +495,7 @@ def tile_attention_prop_pa_kernel(tc, x, w1, b1, w2, b2, gamma, beta, out):
         moments_on_vector(2)
         leaky2(3, 0)
         leaky2(3, 1)
+        weigh_mean(2, vector)
         invert_deviation(2, 1.0)
         gain_and_shift(2, gpsimd)
         stats_on_vector(3, 0)
@@ -484,23 +503,23 @@ def tile_attention_prop_pa_kernel(tc, x, w1, b1, w2, b2, gamma, beta, out):
 
         for chunk in (0, 1):
             for half in (0, 1):
-                transpose_out(chunk, half)
-        copy_and_store(0, 0, scalar)
-        copy_and_store(0, 1, scalar)
-        copy_and_store(1, 0, scalar)
+                transpose_out(chunk, 4 * half, 4)
+        copy_and_store(0, 0, 4, scalar)
+        copy_and_store(0, 4, 4, scalar)
+        copy_and_store(1, 0, 4, scalar)
         normalise(2, 0, gpsimd)
         normalise(2, 1, vector)
         moments_on_vector(3)
-        copy_and_store(1, 1, vector)
         invert_deviation(3, 1.0)
+        weigh_mean(3, vector)
+        copy_and_store(1, 4, 4, vector)
         gain_and_shift(3, vector)
-        transpose_out(2, 0)
-        transpose_out(2, 1)
-        copy_and_store(2, 0, scalar)
-        copy_and_store(2, 1, scalar)
-        normalise(3, 0, vector)
-        normalise(3, 1, vector)
-        transpose_out(3, 0)
-        transpose_out(3, 1)
-        copy_and_store(3, 0, vector)
-        copy_and_store(3, 1, scalar)
+        transpose_out(2, 0, 4)
+        transpose_out(2, 4, 4)
+        copy_and_store(2, 0, 4, scalar)
+        copy_and_store(2, 4, 4, scalar)
+        for quarter in range(4):
+            normalise(3, None, vector, quarter)
+            transpose_out(3, 2 * quarter, 2)
+        for quarter in range(4):
+            copy_and_store(3, 2 * quarter, 2, vector if quarter % 2 == 0 else scalar)

from contextlib import ExitStack

import concourse.mybir as mybir
from concourse.masks import make_identity

F32 = mybir.dt.float32
BF16 = mybir.dt.bfloat16
U32 = mybir.dt.uint32
U8 = mybir.dt.uint8
FP8X4 = mybir.dt.float8_e4m3fn_x4
ALU = mybir.AluOpType
ACT = mybir.ActivationFunctionType

P = 128
ROWS = 1024
WIDTH = 512
PACK = 4
STRIPES = ROWS // P
PIECE = 256
HALF = 512
HALVES = ROWS // HALF
QUARTER = 256
W1_COLS = 256
W1_PART = 256
RUN = 4
BN_STATS_SIZE = 6
BANKS = 8
EPS = 1e-5
SLOPE = 0.01

FLOPS = 2 * 2 * ROWS * WIDTH * WIDTH


def tile_attention_prop_pa_kernel(tc, x, w1, b1, w2, b2, gamma, beta, out):
    nc = tc.nc
    with ExitStack() as ctx:
        sbuf = ctx.enter_context(tc.tile_pool(name="sbuf", bufs=1))
        psum = ctx.enter_context(tc.psum_pool(name="psum", bufs=1))
        ctx.enter_context(tc.manual_schedule())

        banks_taken = [0]

        def next_bank(shape, name):
            tag = "bank%d" % (banks_taken[0] % BANKS)
            banks_taken[0] = banks_taken[0] + 1
            return psum.tile(shape, F32, tag=tag, name=name)

        b1_col = sbuf.tile([P, PACK], BF16, name="b1_col")
        rest_rows = sbuf.tile([P, P], BF16, name="rest_rows")
        nc.vector.memset(rest_rows[:], 0.0)
        one = sbuf.tile([P, 1], F32, name="one")
        nc.vector.memset(one[:], 1.0)
        nc.scalar.dma_start(out=b1_col[:], in_=b1.rearrange("(p t) -> p t", t=PACK))
        table_warmer = sbuf.tile([P, 1], F32, name="table_warmer")
        nc.scalar.activation(out=table_warmer[:], in_=one[:], func=ACT.Abs_reciprocal_sqrt)
        identity = sbuf.tile([P, P], F32, name="identity")
        make_identity(nc, identity[:])
        for r, values in enumerate((b2, gamma, beta)):
            nc.gpsimd.dma_start(
                out=rest_rows[PACK * r : PACK * (r + 1), :], in_=values.rearrange("(t p) -> t p", p=P)
            )

        x_view = x.rearrange("(i c) k -> i (c k)", c=STRIPES)
        stripes_in_piece = PIECE // P
        x_share = stripes_in_piece * WIDTH
        w_view = {
            "w1l": w1.rearrange("(p t) f -> p t f", t=PACK)[:, :, 0:W1_COLS],
            "w1r": w1.rearrange("(p t) f -> p t f", t=PACK)[:, :, W1_COLS:WIDTH],
            "w2": w2.rearrange("(p t) f -> p t f", t=PACK),
        }
        w_width = {"w1l": W1_COLS, "w1r": WIDTH - W1_COLS, "w2": WIDTH}
        x_raw = {}
        w_raw = {}

        def load_x(piece):
            x_raw[piece] = sbuf.tile([P, x_share], BF16, name="x_raw%d" % piece)
            nc.sync.dma_start(out=x_raw[piece][:], in_=x_view[:, x_share * piece : x_share * (piece + 1)])

        def load_w(part):
            w_raw[part] = sbuf.tile([P, PACK, w_width[part]], BF16, name="raw_" + part)
            nc.sync.dma_start(out=w_raw[part][:], in_=w_view[part])

        load_x(0)
        load_w("w1l")
        load_w("w1r")
        load_x(1)
        load_w("w2")
        load_x(2)
        load_x(3)

        w1_words = sbuf.tile([P, WIDTH], U32, align_bytes=64, name="w1_words")
        w1_plane = sbuf.tile([P, WIDTH], U8, align_bytes=64, name="w1_plane")
        w2_words = sbuf.tile([P, WIDTH], U32, align_bytes=64, name="w2_words")
        w2_plane = sbuf.tile([P, WIDTH], U8, align_bytes=64, name="w2_plane")
        x_words = sbuf.tile([P, ROWS], U32, align_bytes=64, name="x_words")
        x_plane = sbuf.tile([P, ROWS], U8, align_bytes=64, name="x_plane")
        h1_words = sbuf.tile([P, ROWS], U32, align_bytes=64, name="h1_words")
        h1_plane = sbuf.tile([P, ROWS], U8, align_bytes=64, name="h1_plane")
        w1_grouped = sbuf.tile([P, WIDTH, PACK], BF16, align_bytes=64, name="w1_grouped")
        w2_grouped = sbuf.tile([P, WIDTH, PACK], BF16, align_bytes=64, name="w2_grouped")
        w_packed = {
            "w1a": (w1_words[:, 0:W1_PART], w1_plane[:, 0:W1_PART], w1_grouped[:, 0:W1_PART, :]),
            "w1b": (w1_words[:, W1_PART:WIDTH], w1_plane[:, W1_PART:WIDTH], w1_grouped[:, W1_PART:WIDTH, :]),
            "w2": (w2_words[:], w2_plane[:], w2_grouped[:]),
        }

        def regroup_w1(part):
            ms = {"w1l": slice(0, P // 2), "w1r": slice(P // 2, P)}[part]
            nc.vector.tensor_copy(
                out=w1_grouped[:].rearrange("p (t m) k -> p t m k", t=PACK)[:, :, ms, :],
                in_=w_raw[part][:].rearrange("p k (m t) -> p t m k", t=PACK),
            )

        def regroup_w2():
            nc.vector.tensor_copy(
                out=w2_grouped[:].rearrange("p (b r) t -> p b t r", r=RUN),
                in_=w_raw["w2"][:].rearrange("p t (b r) -> p b t r", r=RUN),
            )

        def quantise_w(part):
            words, plane, grouped = w_packed[part]
            nc.vector.quantize_mx(
                out=words.bitcast(FP8X4), scales=plane, in_=grouped.rearrange("p f t -> p (f t)")
            )

        x_bank = {}
        x_grouped = {}

        def transpose_x(piece):
            x_bank[piece] = next_bank([P, stripes_in_piece, 2, P], "x_bank%d" % piece)
            x_as_f32 = x_raw[piece][:].bitcast(F32).rearrange("i (c p u) -> i c u p", c=stripes_in_piece, u=2)
            for c in range(stripes_in_piece):
                for u in range(2):
                    nc.tensor.transpose(x_bank[piece][:, c, u, :], x_as_f32[:, c, u, :], identity[:])

        def copy_x(piece):
            x_grouped[piece] = sbuf.tile([P, PACK * PIECE], BF16, align_bytes=64, name="x_grouped%d" % piece)
            nc.scalar.copy(
                out=x_grouped[piece][:].bitcast(F32).rearrange("p (c i u) -> p c i u", c=stripes_in_piece, u=2),
                in_=x_bank[piece][:].rearrange("p c u i -> p c i u"),
            )

        def piece_columns(piece):
            return slice(PIECE * piece, PIECE * (piece + 1))

        def quantise_x(piece):
            cols = piece_columns(piece)
            nc.vector.quantize_mx(
                out=x_words[:, cols].bitcast(FP8X4), scales=x_plane[:, cols], in_=x_grouped[piece][:]
            )

        small_bank = {}

        rest_f32 = sbuf.tile([P, P], F32, name="rest_f32")
        rest_col = sbuf.tile([P, 3 * PACK], F32, name="rest_col")
        b2_most = sbuf.tile([P, PACK], F32, name="b2_most")
        centre = sbuf.tile([P, PACK], F32, name="centre")

        def gamma_col(chunk):
            return rest_col[:, PACK + chunk : PACK + chunk + 1]

        def beta_col(chunk):
            return rest_col[:, 2 * PACK + chunk : 2 * PACK + chunk + 1]

        def cast_rest():
            nc.scalar.copy(out=rest_f32[:], in_=rest_rows[:])

        def transpose_rest():
            small_bank["rest"] = next_bank([P, P], "rest_bank")
            nc.tensor.transpose(small_bank["rest"][:], rest_f32[:], identity[:])

        def derive_rest():
            nc.scalar.copy(out=rest_col[:], in_=small_bank["rest"][:, 0 : 3 * PACK])
            nc.scalar.mul(out=b2_most[:], in_=rest_col[:, 0:PACK], mul=1.0 - SLOPE)
            nc.scalar.activation(out=centre[:], in_=rest_col[:, 0:PACK], func=ACT.Relu, scale=1.0 - SLOPE)

        l1_bank = {}
        v = {}
        h1_grouped = {}

        def layer1(piece, pair):
            cols = piece_columns(piece)
            l1_bank[piece, pair] = next_bank([P, 2, PIECE], "l1_bank%d_%d" % (piece, pair))
            for e in range(2):
                features = slice(P * (2 * pair + e), P * (2 * pair + e + 1))
                nc.tensor.matmul_mx(
                    out=l1_bank[piece, pair][:, e, :],
                    lhsT=w1_words[:, features].bitcast(FP8X4),
                    lhsT_scale=w1_plane[:, features],
                    rhs=x_words[:, cols].bitcast(FP8X4),
                    rhs_scale=x_plane[:, cols],
                    start=True,
                    stop=True,
                )

        def add_b1(piece):
            v[piece] = sbuf.tile([P, PACK, PIECE], F32, name="v%d" % piece)
            for t in range(PACK):
                nc.scalar.activation(
                    out=v[piece][:, t, :],
                    in_=l1_bank[piece, t // 2][:, t % 2, :],
                    func=ACT.Identity,
                    bias=b1_col[:, t : t + 1],
                    scale=1.0,
                )

        def leaky1(piece):
            h1_grouped[piece] = sbuf.tile([P, PIECE, PACK], BF16, align_bytes=64, name="h1_grouped%d" % piece)
            by_row = v[piece][:].rearrange("p t n -> p n t")
            nc.vector.scalar_tensor_tensor(
                out=h1_grouped[piece][:], in0=by_row, scalar=SLOPE, in1=by_row, op0=ALU.mult, op1=ALU.max
            )

        def quantise_h1(piece):
            cols = piece_columns(piece)
            nc.vector.quantize_mx(
                out=h1_words[:, cols].bitcast(FP8X4),
                scales=h1_plane[:, cols],
                in_=h1_grouped[piece][:].rearrange("p n t -> p (n t)"),
            )

        def half_columns(half):
            return slice(HALF * half, HALF * (half + 1))

        l2_bank = {}
        sloped = {}
        q = {}

        def layer2(chunk, half):
            features = slice(P * chunk, P * (chunk + 1))
            cols = half_columns(half)
            l2_bank[chunk, half] = next_bank([P, HALF], "l2_bank%d_%d" % (chunk, half))
            nc.tensor.matmul_mx(
                out=l2_bank[chunk, half][:],
                lhsT=w2_words[:, features].bitcast(FP8X4),
                lhsT_scale=w2_plane[:, features],
                rhs=h1_words[:, cols].bitcast(FP8X4),
                rhs_scale=h1_plane[:, cols],
                start=True,
                stop=True,
            )

        def slope2(chunk, half):
            sloped[chunk, half] = sbuf.tile([P, HALF], F32, name="sloped%d_%d" % (chunk, half))
            nc.scalar.mul(out=sloped[chunk, half][:], in_=l2_bank[chunk, half][:], mul=SLOPE)

        def leaky2(chunk, half, row_sum=None):
            if chunk not in q:
                q[chunk] = sbuf.tile([P, ROWS], F32, name="q%d" % chunk)
            nc.vector.scalar_tensor_tensor(
                out=q[chunk][:, half_columns(half)],
                in0=l2_bank[chunk, half][:],
                scalar=b2_most[:, chunk : chunk + 1],
                in1=sloped[chunk, half][:],
                op0=ALU.add,
                op1=ALU.max,
                accum_out=row_sum,
            )

        half_stats = {}
        moments = {}

        def stats_on_vector(chunk, half):
            if chunk not in half_stats:
                half_stats[chunk] = sbuf.tile([P, HALVES, BN_STATS_SIZE], F32, name="half_stats%d" % chunk)
            nc.vector.bn_stats(out=half_stats[chunk][:, half, :], in_=q[chunk][:, half_columns(half)])

        def moments_on_vector(chunk):
            moments[chunk] = sbuf.tile([P, 2], F32, name="moments%d" % chunk)
            nc.vector.bn_aggr(out=moments[chunk][:], in_=half_stats[chunk][:].rearrange("p h s -> p (h s)"))

        sums = sbuf.tile([P, HALVES], F32, name="sums")
        squares = sbuf.tile([P, HALVES], F32, name="squares")

        def squares_on_scalar(chunk, half):
            unused = sbuf.tile([P, HALF], BF16, name="unused%d" % half)
            nc.scalar.activation(
                out=unused[:],
                in_=q[chunk][:, half_columns(half)],
                func=ACT.Square,
                bias=centre[:, chunk : chunk + 1],
                scale=-1.0,
                accum_out=squares[:, half : half + 1],
            )

        def moments_on_gpsimd(chunk):
            moments[chunk] = sbuf.tile([P, 2], F32, name="moments%d" % chunk)
            work = sbuf.tile([P, 2], F32, name="moments_work")
            nc.gpsimd.tensor_scalar(
                out=moments[chunk][:, 0:1],
                in0=sums[:, 0:1],
                scalar1=sums[:, 1:2],
                scalar2=1.0 / ROWS,
                op0=ALU.add,
                op1=ALU.mult,
            )
            nc.gpsimd.tensor_scalar(
                out=work[:, 0:1],
                in0=squares[:, 0:1],
                scalar1=squares[:, 1:2],
                scalar2=1.0 / ROWS,
                op0=ALU.add,
                op1=ALU.mult,
            )
            nc.gpsimd.tensor_scalar(
                out=work[:, 1:2],
                in0=moments[chunk][:, 0:1],
                scalar1=centre[:, chunk : chunk + 1],
                scalar2=0.0,
                op0=ALU.subtract,
                op1=ALU.add,
            )
            nc.gpsimd.tensor_scalar(
                out=moments[chunk][:, 1:2],
                in0=work[:, 1:2],
                scalar1=work[:, 1:2],
                scalar2=work[:, 0:1],
                op0=ALU.mult,
                op1=ALU.subtract,
            )

        inverse_deviation = {}
        mean_gamma = {}
        gain = {}
        shift = {}

        def weigh_mean(chunk, engine):
            mean_gamma[chunk] = sbuf.tile([P, 1], F32, name="mean_gamma%d" % chunk)
            engine.tensor_scalar(
                out=mean_gamma[chunk][:],
                in0=moments[chunk][:, 0:1],
                scalar1=gamma_col(chunk),
                scalar2=-1.0,
                op0=ALU.mult,
                op1=ALU.mult,
            )

        def invert_deviation(chunk, variance_sign):
            inverse_deviation[chunk] = sbuf.tile([P, 1], F32, name="inverse_deviation%d" % chunk)
            nc.scalar.activation(
                out=inverse_deviation[chunk][:],
                in_=moments[chunk][:, 1:2],
                func=ACT.Abs_reciprocal_sqrt,
                bias=EPS,
                scale=variance_sign,
            )

        def gain_and_shift(chunk, engine):
            gain[chunk] = sbuf.tile([P, 1], F32, name="gain%d" % chunk)
            shift[chunk] = sbuf.tile([P, 1], F32, name="shift%d" % chunk)
            engine.tensor_scalar(
                out=gain[chunk][:],
                in0=gamma_col(chunk),
                scalar1=inverse_deviation[chunk][:],
                scalar2=0.0,
                op0=ALU.mult,
                op1=ALU.add,
            )
            engine.tensor_scalar(
                out=shift[chunk][:],
                in0=mean_gamma[chunk][:],
                scalar1=inverse_deviation[chunk][:],
                scalar2=beta_col(chunk),
                op0=ALU.mult,
                op1=ALU.add,
            )

        y = {}

        def normalise(chunk, half, engine, quarter=None):
            if chunk not in y:
                y[chunk] = sbuf.tile([P, ROWS], F32, name="y%d" % chunk)
            cols = half_columns(half) if quarter is None else slice(QUARTER * quarter, QUARTER * (quarter + 1))
            if engine is nc.scalar:
                engine.activation(
                    out=y[chunk][:, cols],
                    in_=q[chunk][:, cols],
                    func=ACT.Identity,
                    bias=shift[chunk][:],
                    scale=gain[chunk][:],
                )
            else:
                engine.tensor_scalar(
                    out=y[chunk][:, cols],
                    in0=q[chunk][:, cols],
                    scalar1=gain[chunk][:],
                    scalar2=shift[chunk][:],
                    op0=ALU.mult,
                    op1=ALU.add,
                )

        out_bank = {}
        out_view = out.rearrange("(i c) f -> i c f", c=STRIPES)

        def transpose_out(chunk, first, count):
            out_bank[chunk, first] = next_bank([P, count, P], "out_bank%d_%d" % (chunk, first))
            for c in range(count):
                row = P * (first + c)
                nc.tensor.transpose(out_bank[chunk, first][:, c, :], y[chunk][:, row : row + P], identity[:])

        def copy_and_store(chunk, first, count, engine):
            rows = sbuf.tile([P, count, P], F32, name="rows%d_%d" % (chunk, first))
            if engine is nc.scalar:
                engine.copy(out=rows[:], in_=out_bank[chunk, first][:])
            else:
                engine.tensor_copy(out=rows[:], in_=out_bank[chunk, first][:])
            nc.sync.dma_start(
                out=out_view[:, first : first + count, P * chunk : P * (chunk + 1)], in_=rows[:]
            )

        scalar, vector, gpsimd = nc.scalar, nc.vector, nc.gpsimd

        transpose_x(0)
        copy_x(0)
        regroup_w1("w1l")
        regroup_w1("w1r")
        quantise_x(0)
        quantise_w("w1a")
        quantise_w("w1b")
        transpose_x(1)
        copy_x(1)
        regroup_w2()
        quantise_x(1)
        layer1(0, 0)
        layer1(0, 1)
        add_b1(0)
        quantise_w("w2")
        transpose_x(2)
        copy_x(2)
        layer1(1, 0)
        layer1(1, 1)
        leaky1(0)
        add_b1(1)
        quantise_x(2)
        quantise_h1(0)
        transpose_x(3)
        copy_x(3)
        layer1(2, 0)
        layer1(2, 1)
        add_b1(2)
        leaky1(1)
        quantise_x(3)
        quantise_h1(1)
        layer1(3, 0)
        layer1(3, 1)
        add_b1(3)
        leaky1(2)
        leaky1(3)
        quantise_h1(2)
        quantise_h1(3)

        cast_rest()
        layer2(0, 0)
        layer2(1, 0)
        transpose_rest()
        slope2(0, 0)
        derive_rest()
        slope2(1, 0)
        layer2(2, 0)
        slope2(2, 0)
        leaky2(0, 0)
        leaky2(1, 0, row_sum=sums[:, 0:1])
        stats_on_vector(0, 0)
        layer2(0, 1)
        layer2(1, 1)
        slope2(0, 1)
        slope2(1, 1)
        leaky2(0, 1)
        leaky2(1, 1, row_sum=sums[:, 1:2])
        stats_on_vector(0, 1)
        squares_on_scalar(1, 0)
        layer2(2, 1)
        slope2(2, 1)
        squares_on_scalar(1, 1)
        leaky2(2, 0)
        moments_on_vector(0)
        leaky2(2, 1)
        weigh_mean(0, vector)
        moments_on_gpsimd(1)
        weigh_mean(1, gpsimd)
        invert_deviation(0, 1.0)
        gain_and_shift(0, vector)
        stats_on_vector(2, 0)
        stats_on_vector(2, 1)
        layer2(3, 0)
        slope2(3, 0)
        normalise(0, 0, scalar)
        normalise(0, 1, gpsimd)
        invert_deviation(1, -1.0)
        gain_and_shift(1, vector)
        layer2(3, 1)
        slope2(3, 1)
        normalise(1, 0, scalar)
        normalise(1, 1, gpsimd)
        moments_on_vector(2)
        leaky2(3, 0)
        leaky2(3, 1)
        weigh_mean(2, vector)
        invert_deviation(2, 1.0)
        gain_and_shift(2, gpsimd)
        stats_on_vector(3, 0)
        stats_on_vector(3, 1)

        for chunk in (0, 1):
            for half in (0, 1):
                transpose_out(chunk, 4 * half, 4)
        copy_and_store(0, 0, 4, scalar)
        copy_and_store(0, 4, 4, scalar)
        copy_and_store(1, 0, 4, scalar)
        normalise(2, 0, gpsimd)
        normalise(2, 1, vector)
        moments_on_vector(3)
        invert_deviation(3, 1.0)
        weigh_mean(3, vector)
        copy_and_store(1, 4, 4, vector)
        gain_and_shift(3, vector)
        transpose_out(2, 0, 4)
        transpose_out(2, 4, 4)
        copy_and_store(2, 0, 4, scalar)
        copy_and_store(2, 4, 4, scalar)
        for quarter in range(4):
            normalise(3, None, vector, quarter)
            transpose_out(3, 2 * quarter, 2)
        for quarter in range(4):
            copy_and_store(3, 2 * quarter, 2, vector if quarter % 2 == 0 else scalar)
